import numpy as np
import ml_dtypes


def mxq(x, axis, fmt="e4m3"):
    dtype, down = {"e4m3": (ml_dtypes.float8_e4m3fn, 7), "e5m2": (ml_dtypes.float8_e5m2, 14)}[fmt]
    v = np.moveaxis(np.asarray(x, np.float32).astype(ml_dtypes.bfloat16).astype(np.float64), axis, -1)
    blocks = v.reshape(v.shape[:-1] + (-1, 32))
    amax = np.abs(blocks).max(-1, keepdims=True)
    byte = np.maximum(np.where(amax > 0, np.frexp(amax)[1] - 1 + 127, 0) - down, 1)
    scale = np.exp2(byte - 127.0)
    codes = (blocks / scale).astype(np.float32).astype(dtype).astype(np.float64)
    return np.moveaxis((codes * scale).reshape(v.shape), -1, axis)


WIDE = False


def mx_kscale(k):
    if not WIDE:
        return np.ones(k)
    levels = np.array([18, -18])
    if k % 512:
        return np.exp2(np.random.permutation(np.resize(levels, k // 32))).repeat(32)
    a = np.empty((k // 512, 16))
    for p in range(k // 512):
        a[p, :8] = np.random.permutation(np.resize(levels, 8))
        for g in range(8):
            far = levels[np.abs(levels - a[p, g]) >= 10]
            a[p, g + 8] = far[np.random.randint(len(far))]
    return np.exp2(a.ravel()).repeat(32)


BF16 = ml_dtypes.bfloat16


def bf(x):
    return np.asarray(x, np.float32).astype(BF16)


def f64(x):
    return np.asarray(x).astype(np.float64)


B, S, E, H, HD = 1, 512, 1024, 8, 256
V = H * HD
T = B * S
EPS = 1e-5


def sigmoid(v):
    return 1.0 / (1.0 + np.exp(-v))


def setup_inputs():
    s = mx_kscale(T)[:, None]
    u = mx_kscale(E)
    v = mx_kscale(V)
    lvl = np.exp2(np.random.uniform(-9.0, 2.0, (B, S, H, 1)))
    x0 = bf(np.random.standard_normal((B, S, E)))
    wg0 = bf(np.random.standard_normal((E, V)) / np.sqrt(E))
    ret = bf(np.random.standard_normal((B, S, H, HD)) * lvl)
    wo0 = bf(np.random.standard_normal((V, E)) * 1.5 / np.sqrt(V))
    noise = np.random.standard_normal((T, E)) * np.exp2(np.random.randint(-6, 1, (T, 1)))
    g = bf((2.0 * noise / s * u).reshape(B, S, E))
    gate = (f64(x0).reshape(T, E) @ f64(wg0)).reshape(B, S, V)
    r = f64(ret)
    rstd = 1.0 / np.sqrt(np.mean(r * r, axis=-1, keepdims=True) + EPS)
    return {"x": bf((f64(x0).reshape(T, E) * s).reshape(B, S, E)),
            "wg": bf(f64(wg0) / v),
            "ret": ret,
            "wo": bf(f64(wo0) * v[:, None] / u),
            "gate": np.asarray(gate, np.float32),
            "rstd": np.asarray(rstd, np.float32),
            "grad_out": g}


def reference(x, wg, ret, wo, gate, rstd, grad_out):
    gf = f64(gate).reshape(T, V)
    sg = sigmoid(gf)
    n = (f64(ret) * f64(rstd)).reshape(T, V)
    go = f64(grad_out).reshape(T, E)
    dh = mxq(go, 1, "e5m2") @ mxq(f64(wo), 1, "e4m3").T
    dgate = dh * n * (sg * (1.0 + gf * (1.0 - sg)))
    dx = mxq(dgate, 1, "e5m2") @ mxq(f64(wg), 1, "e4m3").T
    dwg = mxq(f64(x).reshape(T, E), 0, "e4m3").T @ mxq(dgate, 0, "e5m2")
    return dx.reshape(B, S, E), dwg

from contextlib import ExitStack

import concourse.mybir as mybir
from concourse.masks import make_identity

F32 = mybir.dt.float32
BF16 = mybir.dt.bfloat16
U32 = mybir.dt.uint32
U8 = mybir.dt.uint8
E4M3 = mybir.dt.float8_e4m3fn_x4
E5M2 = mybir.dt.float8_e5m2_x4
ADD = mybir.AluOpType.add
MULT = mybir.AluOpType.mult
TANH = mybir.ActivationFunctionType.Tanh
SILU = mybir.ActivationFunctionType.Silu

TOKENS, FEATURES, GATES, HEADS = 512, 1024, 2048, 8
FLOPS = 3 * 2 * TOKENS * FEATURES * GATES

P = 128
SLOTS = 4
WIDTH = 512
CHUNKS = GATES // WIDTH
HALF = GATES // 2
HEAD = GATES // HEADS
WG_PARTS = FEATURES // WIDTH

BANKS = {"turn": 3, "dh": 2, "out": 3}
OUT0_BANKS = (("dh", "dh"), ("turn", "turn"), ("out", "out"), ("dh", "dh"))

LOADS = (
    ("x", ()), ("grad_out", (0,)), ("grad_out", (1,)), ("rstd", ()), ("wo", (0, 0)), ("gate", (0, 1)),
    ("gate", (0, 0)), ("wo", (0, 1)), ("ret", (0, 0)), ("gate", (0, 2)), ("gate", (0, 3)), ("ret", (0, 1)),
    ("wo", (1, 0)), ("wo", (1, 1)), ("wg", (0,)), ("wg", (1,)), ("gate", (1, 0)), ("wo", (3, 0)), ("gate", (1, 1)),
    ("wo", (2, 0)), ("ret", (1, 0)), ("wo", (2, 1)), ("gate", (1, 3)), ("wg", (3,)), ("gate", (1, 2)),
    ("ret", (1, 1)), ("wo", (3, 1)), ("wg", (2,)),
)

ONCE = ("turn_go", "lay_go", "quantise_go", "lay_x", "quantise_x", "scale_rstd", "begin_out0", "end_out0", "store_out0")
PLAN = (
    ("lay_x", (0,), 0, ""),
    ("quantise_x", (0,), 0, ""),
    ("turn_go", (0, 1), 0, ""),
    ("turn_go", (0, 0), 0, ""),
    ("lay_go", (0, 0), 0, "S"),
    ("turn_go", (1, 0), 0, ""),
    ("lay_x", (1,), 0, ""),
    ("lay_go", (0, 1), 0, "V"),
    ("lay_go", (1, 0), 0, "S"),
    ("quantise_x", (1,), 0, ""),
    ("turn_go", (1, 1), 0, ""),
    ("lay_go", (1, 1), 0, "S"),
    ("scale_rstd", (), 0, ""),
    ("quantise_go", (0,), 0, ""),
    ("quantise_go", (1,), 0, ""),
    ("lay_wg", (1, 1), 4, "SSSS"),
    ("quantise_wg", (0,), 4, ""),
    ("multiply_out1", (0,), 4, ""),
    ("multiply_out1", (1,), 4, ""),
    ("make_b", (1,), 3, ""),
    ("lay_wo", (0, 0), 2, "VSSS"),
    ("multiply_out1", (2,), 4, ""),
    ("store_out1", (0,), 4, "SSSS"),
    ("turn_wo", (0, 1), 2, ""),
    ("turn_wo", (1, 1), 2, ""),
    ("lay_wo", (0, 1), 2, "VSSS"),
    ("quantise_dt", (1,), 4, ""),
    ("turn_wo", (1, 0), 2, ""),
    ("turn_wg", (0, 0), 3, ""),
    ("make_q", (0,), 2, ""),
    ("turn_dt", (0,), 3, ""),
    ("make_dgate", (2,), 3, ""),
    ("lay_wo", (1, 1), 2, "SSSS"),
    ("begin_out0", (0, 1), 7, ""),
    ("turn_wg", (1, 0), 3, ""),
    ("lay_wo", (1, 0), 2, "SSSS"),
    ("lay_wg", (0, 0), 3, "SVSS"),
    ("store_out1", (1,), 4, "SSSV"),
    ("make_dgate", (3,), 3, ""),
    ("store_out1", (2,), 4, "SSSS"),
    ("turn_wg", (0, 1), 3, ""),
    ("quantise_wo", (), 2, ""),
    ("lay_dt", (0,), 3, "SSSS"),
    ("multiply_out1", (3,), 4, ""),
    ("activate", (1,), 2, ""),
    ("multiply_out1", (4,), 4, ""),
    ("quantise_wg", (1,), 4, ""),
    ("multiply_out1", (5,), 4, ""),
    ("multiply_dh", (0,), 2, ""),
    ("lay_wg", (1, 0), 3, "SSSS"),
    ("lay_wg", (0, 1), 3, "SVSS"),
    ("store_out1", (3,), 4, "SSVS"),
    ("lay_dg", (), 3, ""),
    ("begin_out0", (0, 0), 6, ""),
    ("store_out1", (4,), 4, "SSSS"),
    ("begin_out0", (1, 1), 7, ""),
    ("make_b", (0,), 2, ""),
    ("multiply_dh", (1,), 2, ""),
    ("turn_dt", (1,), 3, ""),
    ("make_q", (1,), 2, ""),
    ("turn_wg", (1, 1), 3, ""),
    ("store_out1", (5,), 4, "SSSS"),
    ("activate", (0,), 1, ""),
    ("turn_wo", (0, 0), 1, ""),
    ("make_dgate", (0,), 2, ""),
    ("multiply_out1", (6,), 4, ""),
    ("make_dgate", (1,), 2, ""),
    ("quantise_dt", (0,), 3, ""),
    ("store_out1", (6,), 4, "SSSS"),
    ("end_out0", (0, 0), 7, ""),
    ("multiply_out1", (7,), 4, ""),
    ("begin_out0", (1, 0), 6, ""),
    ("multiply_dh", (2,), 2, ""),
    ("quantise_dg", (), 3, ""),
    ("multiply_dh", (3,), 2, ""),
    ("store_out1", (7,), 4, "SSVV"),
    ("lay_dt", (1,), 3, "SSSS"),
    ("end_out0", (1, 0), 8, ""),
    ("end_out0", (0, 1), 8, ""),
    ("begin_out0", (2, 1), 8, ""),
    ("store_out0", (0, 0), 8, "S"),
    ("store_out0", (0, 1), 8, "S"),
    ("end_out0", (2, 1), 8, ""),
    ("begin_out0", (2, 0), 8, ""),
    ("end_out0", (2, 0), 8, ""),
    ("begin_out0", (3, 1), 8, ""),
    ("store_out0", (2, 0), 8, "S"),
    ("store_out0", (2, 1), 8, "V"),
    ("end_out0", (1, 1), 8, ""),
    ("end_out0", (3, 1), 8, ""),
    ("begin_out0", (3, 0), 8, ""),
    ("store_out0", (1, 0), 8, "V"),
    ("store_out0", (1, 1), 8, "V"),
    ("end_out0", (3, 0), 8, ""),
    ("store_out0", (3, 0), 8, "S"),
    ("store_out0", (3, 1), 8, "V"),
)


def tile_retnet_pc_v_kernel(tc, x, wg, ret, wo, gate, rstd, grad_out, out_0, out_1):
    nc = tc.nc
    x_v = x.rearrange("b (p j) e -> p (b j) e", j=SLOTS)
    go_v = grad_out.rearrange("b (p j) e -> p (b j) e", j=SLOTS)
    gate_v = gate.rearrange("b (p j) v -> p (b j) v", j=SLOTS)
    ret_v = ret.rearrange("b (p j) h d -> p (b j) (h d)", j=SLOTS)
    rstd_v = rstd.rearrange("b (p j) h o -> p (b j) (h o)", j=SLOTS)
    wo_v = wo.rearrange("(c b p r) e -> c p b r e", b=2, p=P, r=2)
    wg_v = wg.rearrange("(b p r) v -> b p r v", p=P, r=2)
    out0_v = out_0.rearrange("b (p j) e -> p (b j) e", j=SLOTS)
    out1_v = out_1.rearrange("(i p) v -> p i v", p=P)

    with ExitStack() as ctx:
        keep = ctx.enter_context(tc.tile_pool(name="keep", bufs=1))
        flow = ctx.enter_context(tc.tile_pool(name="flow", bufs=1))
        psum = ctx.enter_context(tc.psum_pool(name="psum", bufs=1))

        identity = keep.tile([P, P], F32, name="identity")
        make_identity(nc, identity[:])
        first = keep.tile([P, 1], F32, name="first")
        nc.gpsimd.memset(first[:], 0.0)
        nc.scalar.activation(out=first[:], in_=first[:], func=SILU)

        go_q = [keep.tile([P, TOKENS], U32, name="go_q%d" % g, align_bytes=64) for g in range(2)]
        go_s = [keep.tile([P, TOKENS], U8, name="go_s%d" % g, align_bytes=64) for g in range(2)]
        x_q = keep.tile([P, FEATURES], U32, name="x_q", align_bytes=64)
        x_s = keep.tile([P, FEATURES], U8, name="x_s", align_bytes=64)
        wg_q = [keep.tile([P, FEATURES], U32, name="wg_q%d" % c, align_bytes=64) for c in range(CHUNKS)]
        wg_s = [keep.tile([P, FEATURES], U8, name="wg_s%d" % c, align_bytes=64) for c in range(CHUNKS)]
        dt_q = [keep.tile([P, TOKENS], U32, name="dt_q%d" % c, align_bytes=64) for c in range(CHUNKS)]
        dt_s = [keep.tile([P, TOKENS], U8, name="dt_s%d" % c, align_bytes=64) for c in range(CHUNKS)]
        rstd_raw = keep.tile([P, SLOTS, HEADS], F32, name="rstd_raw")
        rstd_scale = keep.tile([P, SLOTS, HEADS], F32, name="rstd_scale")

        go_raw, wo_raw, wg_raw, x_raw, gate_raw, ret_raw = {}, {}, {}, {}, {}, {}
        go_il, wo_il, wg_il, x_il, dg_il, dt_il = {}, {}, {}, {}, {}, {}
        wo_q, wo_s, dg_q, dg_s = {}, {}, {}, {}
        q_factor, b_factor, dgate = {}, {}, {}
        banks, out1_stage, out0_stage = {}, {}, {}

        def load_grad_out(s):
            go_raw[s] = keep.tile([P, 2, FEATURES], BF16, name="rows", bufs=6)
            nc.sync.dma_start(out=go_raw[s][:], in_=go_v[:, 2 * s : 2 * s + 2, :])

        def load_wo(c, b):
            wo_raw[c, b] = keep.tile([P, 2, FEATURES], BF16, name="rows", bufs=6)
            nc.sync.dma_start(out=wo_raw[c, b][:], in_=wo_v[c, :, b])

        def load_wg(b):
            wg_raw[b] = keep.tile([P, 2, GATES], BF16, name="wide", bufs=4)
            nc.sync.dma_start(out=wg_raw[b][:], in_=wg_v[b])

        def load_x():
            x_raw[0] = keep.tile([P, SLOTS, FEATURES], BF16, name="wide", bufs=4)
            nc.sync.dma_start(out=x_raw[0][:], in_=x_v)

        def load_gate(h, j):
            if (h, j // 2) not in gate_raw:
                gate_raw[h, j // 2] = keep.tile([P, 2, HALF], F32, name="gate", bufs=3)
            nc.sync.dma_start(out=gate_raw[h, j // 2][:, j % 2, :], in_=gate_v[:, j, h * HALF : (h + 1) * HALF])

        def load_ret(h, s):
            ret_raw[h, s] = keep.tile([P, 2, HALF], BF16, name="ret", bufs=3)
            nc.sync.dma_start(out=ret_raw[h, s][:], in_=ret_v[:, 2 * s : 2 * s + 2, h * HALF : (h + 1) * HALF])

        def load_rstd():
            nc.sync.dma_start(out=rstd_raw[:], in_=rstd_v)

        def copy(engine, out, in_):
            if engine == "V":
                nc.vector.tensor_copy(out=out, in_=in_)
            else:
                nc.scalar.copy(out=out, in_=in_)

        def new_bank(kind):
            return psum.tile([P, 4, P], F32, name=kind, tag=kind, bufs=BANKS[kind])

        def flat(bank):
            return bank[:].rearrange("p a b -> p (a b)")

        def turn(key, rows, g):
            banks[key] = new_bank("turn")
            for r, row in enumerate(rows):
                words = row.bitcast(F32)[:, 256 * g : 256 * (g + 1)]
                for pair in range(2):
                    nc.tensor.transpose(banks[key][:, 2 * r + pair, :], words[:, pair::2], identity[:])

        def lay(engine, key, out, order):
            words = out.rearrange("p n k -> p (n k)").bitcast(F32)
            bank = banks[key][:].rearrange("p (r u) n -> p r u n", u=2)
            if order == "row by row":
                copy(engine, words.rearrange("p (r n u) -> p r n u", r=2, u=2), bank.rearrange("p r u n -> p r n u"))
            else:
                copy(engine, words.rearrange("p (n r u) -> p n r u", r=2, u=2), bank.rearrange("p r u n -> p n r u"))

        def interleave(out, in_):
            nc.vector.tensor_copy(out=out.rearrange("p (n i) j -> p n j i", i=4), in_=in_.rearrange("p j (n i) -> p n j i", i=4))

        def quantise(codes, scales, values, fmt):
            nc.vector.quantize_mx(out=codes.bitcast(fmt), scales=scales, in_=values.rearrange("p n k -> p (n k)"))

        def turn_go(s, g):
            turn(("go", s, g), [go_raw[s][:, j, :] for j in range(2)], g)

        def lay_go(s, g, engine):
            if not go_il:
                go_il[0] = flow.tile([P, 2, TOKENS, 4], BF16, name="wo_il", bufs=2, align_bytes=64)
            lay(engine, ("go", s, g), go_il[0][:, g, 256 * s : 256 * (s + 1), :], "row by row")

        def quantise_go(g):
            quantise(go_q[g][:], go_s[g][:], go_il[0][:, g], E5M2)

        def turn_wo(c, b, g):
            turn(("wo", c, b, g), [wo_raw[c, b][:, r, :] for r in range(2)], g)

        def lay_wo(c, b, g, engine):
            if c not in wo_il:
                wo_il[c] = flow.tile([P, 2, WIDTH, 4], BF16, name="wo_il", bufs=2, align_bytes=64)
            lay(engine, ("wo", c, b, g), wo_il[c][:, g, 256 * b : 256 * (b + 1), :], "row pairs")

        def quantise_wo(c):
            wo_q[c] = flow.tile([P, 2, WIDTH], U32, name="wo_q", bufs=2, align_bytes=64)
            wo_s[c] = flow.tile([P, 2, WIDTH], U8, name="wo_s", bufs=2, align_bytes=64)
            quantise(wo_q[c][:].rearrange("p g n -> p (g n)"), wo_s[c][:].rearrange("p g n -> p (g n)"),
                     wo_il[c][:].rearrange("p g n k -> p (g n) k"), E4M3)

        def turn_wg(c, k, b):
            part, g = divmod(2 * c + k, CHUNKS)
            turn(("wg", 2 * c + k, b), [wg_raw[2 * part + b][:, r, :] for r in range(2)], g)

        def lay_wg(c, k, b, engine):
            if b == 0:
                wg_il[2 * c + k] = flow.tile([P, WIDTH, 4], BF16, name="wg_il", bufs=2, align_bytes=64)
            lay(engine, ("wg", 2 * c + k, b), wg_il[2 * c + k][:, 256 * b : 256 * (b + 1), :], "row pairs")

        def quantise_wg(c, k):
            part, g = divmod(2 * c + k, CHUNKS)
            cols = slice(WIDTH * part, WIDTH * (part + 1))
            quantise(wg_q[g][:, cols], wg_s[g][:, cols], wg_il[2 * c + k][:], E4M3)

        def lay_x(n):
            x_il[n] = flow.tile([P, WIDTH, 4], BF16, name="wg_il", bufs=2, align_bytes=64)
            interleave(x_il[n][:], x_raw[0][:, :, WIDTH * n : WIDTH * (n + 1)])

        def quantise_x(n):
            cols = slice(WIDTH * n, WIDTH * (n + 1))
            quantise(x_q[:, cols], x_s[:, cols], x_il[n][:], E4M3)

        def scale_rstd():
            nc.vector.tensor_scalar_mul(out=rstd_scale[:], in0=rstd_raw[:], scalar1=-0.5)

        def activate(c, s):
            g = gate_raw[c // 2, s][:, :, WIDTH * (c % 2) : WIDTH * (c % 2 + 1)]
            q_factor[c, s] = flow.tile([P, 2, WIDTH], F32, name="q_factor", bufs=3)
            b_factor[c, s] = flow.tile([P, 2, WIDTH], F32, name="b_factor", bufs=4)
            nc.scalar.activation(out=q_factor[c, s][:], in_=g, func=TANH, scale=0.5)
            nc.scalar.activation(out=b_factor[c, s][:], in_=g, func=SILU, scale=-1.0)

        def make_q(c, s):
            q, r = q_factor[c, s][:], ret_raw[c // 2, s][:, :, WIDTH * (c % 2) : WIDTH * (c % 2 + 1)]
            nc.vector.scalar_tensor_tensor(out=q, in0=q, scalar=1.0, in1=r, op0=ADD, op1=MULT)

        def make_b(c, s):
            b = b_factor[c, s][:]
            nc.vector.scalar_tensor_tensor(out=b, in0=b, scalar=-1.0, in1=q_factor[c, s][:], op0=ADD, op1=MULT)

        def multiply_dh(c, j):
            banks["dh", c, j] = new_bank("dh")
            rows = slice(P * j, P * (j + 1))
            for g in range(2):
                nc.tensor.matmul_mx(out=flat(banks["dh", c, j]), lhsT=go_q[g][:, rows].bitcast(E5M2), lhsT_scale=go_s[g][:, rows],
                                    rhs=wo_q[c][:, g, :].bitcast(E4M3), rhs_scale=wo_s[c][:, g, :], start=(g == 0), stop=(g == 1))

        def make_dgate(c, j):
            if j == 0:
                dgate[c] = flow.tile([P, SLOTS, WIDTH], BF16, name="dgate", bufs=2, align_bytes=64)
            for k in range(WIDTH // HEAD):
                cols = slice(HEAD * k, HEAD * (k + 1))
                head = c * (WIDTH // HEAD) + k
                nc.vector.scalar_tensor_tensor(out=dgate[c][:, j, cols], in0=flat(banks["dh", c, j])[:, cols], scalar=rstd_scale[:, j, head : head + 1],
                                               in1=b_factor[c, j // 2][:, j % 2, cols], op0=MULT, op1=MULT)

        def turn_dt(c, s):
            turn(("dt", c, s), [dgate[c][:, 2 * s + j, :] for j in range(2)], 0)

        def lay_dt(c, s, engine):
            if s == 0:
                dt_il[c] = flow.tile([P, TOKENS, 4], BF16, name="dt_il", bufs=1, align_bytes=64)
            lay(engine, ("dt", c, s), dt_il[c][:, 256 * s : 256 * (s + 1), :], "row by row")

        def quantise_dt(c, s):
            if c == CHUNKS - 1:
                cols = slice(256 * s, 256 * (s + 1))
                quantise(dt_q[c][:, cols], dt_s[c][:, cols], dt_il[c][:, cols, :], E5M2)
            elif s == 1:
                quantise(dt_q[c][:], dt_s[c][:], dt_il[c][:], E5M2)

        def lay_dg(c):
            dg_il[c] = flow.tile([P, WIDTH, 4], BF16, name="dg_il", bufs=1, align_bytes=64)
            interleave(dg_il[c][:], dgate[c][:])

        def quantise_dg(c):
            dg_q[c] = flow.tile([P, WIDTH], U32, name="dg_q", bufs=2, align_bytes=64)
            dg_s[c] = flow.tile([P, WIDTH], U8, name="dg_s", bufs=2, align_bytes=64)
            quantise(dg_q[c][:], dg_s[c][:], dg_il[c][:], E5M2)

        def multiply_out1(c, i):
            cols = slice(P * i, P * (i + 1))
            banks["out1", c, i] = new_bank("out")
            nc.tensor.matmul_mx(out=flat(banks["out1", c, i]), lhsT=x_q[:, cols].bitcast(E4M3), lhsT_scale=x_s[:, cols],
                                rhs=dg_q[c][:].bitcast(E5M2), rhs_scale=dg_s[c][:], start=True, stop=True)

        def store_out1(c, i, engine):
            if i % 2 == 0:
                out1_stage[c] = flow.tile([P, 2, WIDTH], F32, name="stage", bufs=5)
            copy(engine, out1_stage[c][:, i % 2, :], flat(banks["out1", c, i]))
            if i % 2 == 1:
                nc.sync.dma_start(out=out1_v[:, i - 1 : i + 1, WIDTH * c : WIDTH * (c + 1)], in_=out1_stage[c][:])

        def pass_out0(j, n, c):
            rows = slice(P * j, P * (j + 1))
            cols = slice(WIDTH * n, WIDTH * (n + 1))
            nc.tensor.matmul_mx(out=flat(banks["out0", j, n]), lhsT=dt_q[c][:, rows].bitcast(E5M2), lhsT_scale=dt_s[c][:, rows],
                                rhs=wg_q[c][:, cols].bitcast(E4M3), rhs_scale=wg_s[c][:, cols], start=(c == 0), stop=(c == CHUNKS - 1))

        def begin_out0(j, n):
            banks["out0", j, n] = new_bank(OUT0_BANKS[j][n])
            for c in range(CHUNKS - 1):
                pass_out0(j, n, c)

        def end_out0(j, n):
            pass_out0(j, n, CHUNKS - 1)

        def store_out0(j, n, engine):
            if n == 0:
                out0_stage[j] = flow.tile([P, WG_PARTS, WIDTH], F32, name="stage", bufs=5)
            copy(engine, out0_stage[j][:, n, :], flat(banks["out0", j, n]))
            if n == WG_PARTS - 1:
                nc.sync.dma_start(out=out0_v[:, j, :], in_=out0_stage[j][:].rearrange("p n e -> p (n e)"))

        loads = {"grad_out": load_grad_out, "wo": load_wo, "wg": load_wg, "x": load_x, "gate": load_gate, "ret": load_ret, "rstd": load_rstd}
        stages = {
            "turn_go": turn_go, "lay_go": lay_go, "quantise_go": quantise_go,
            "turn_wo": turn_wo, "lay_wo": lay_wo, "quantise_wo": quantise_wo,
            "turn_wg": turn_wg, "lay_wg": lay_wg, "quantise_wg": quantise_wg,
            "lay_x": lay_x, "quantise_x": quantise_x, "scale_rstd": scale_rstd,
            "activate": activate, "make_q": make_q, "make_b": make_b,
            "multiply_dh": multiply_dh, "make_dgate": make_dgate,
            "turn_dt": turn_dt, "lay_dt": lay_dt, "quantise_dt": quantise_dt, "lay_dg": lay_dg, "quantise_dg": quantise_dg,
            "multiply_out1": multiply_out1, "store_out1": store_out1,
            "begin_out0": begin_out0, "end_out0": end_out0, "store_out0": store_out0,
        }
        with tc.manual_schedule():
            for name, args in LOADS:
                loads[name](*args)
            steps = CHUNKS + max(row[2] for row in PLAN)
            for step in range(steps):
                for stage, args, first_step, engines in PLAN:
                    c = step - first_step
                    if stage in ONCE and c == 0:
                        stages[stage](*args, *engines)
                    elif stage not in ONCE and 0 <= c < CHUNKS:
                        stages[stage](c, *args, *engines[c : c + 1])
